import numpy as np
import ml_dtypes


def mxq(x, axis, fmt="e4m3"):
    dtype, down = {"e4m3": (ml_dtypes.float8_e4m3fn, 7), "e5m2": (ml_dtypes.float8_e5m2, 14)}[fmt]
    v = np.moveaxis(np.asarray(x, np.float32).astype(ml_dtypes.bfloat16).astype(np.float64), axis, -1)
    blocks = v.reshape(v.shape[:-1] + (-1, 32))
    amax = np.abs(blocks).max(-1, keepdims=True)
    byte = np.maximum(np.where(amax > 0, np.frexp(amax)[1] - 1 + 127, 0) - down, 1)
    scale = np.exp2(byte - 127.0)
    codes = (blocks / scale).astype(np.float32).astype(dtype).astype(np.float64)
    return np.moveaxis((codes * scale).reshape(v.shape), -1, axis)


WIDE = False


def mx_kscale(k):
    if not WIDE:
        return np.ones(k)
    levels = np.array([10, -10, 5, -5, 0])
    a = np.random.permutation(np.resize(levels, k // 512 * 4)).reshape(k // 512, 4)
    idx = np.arange(k)
    return np.exp2(a[idx // 512, idx % 128 // 32])


BF16 = ml_dtypes.bfloat16


def bf(x):
    return np.asarray(x, np.float32).astype(BF16)


def f64(x):
    return np.asarray(x).astype(np.float64)


B, N, E, F = 4, 1024, 1024, 128


def setup_inputs():
    u = mx_kscale(E)
    t = np.exp2(np.round(np.log2(mx_kscale(N)) / 2))
    g = np.exp2(np.round(np.log2(np.mean(t * t))))
    sign = np.where(np.random.standard_normal(E) < 0.0, -1.0, 1.0)
    return {"node_features": bf(np.random.standard_normal((B, N, F)) * 0.25 * np.sqrt(N) * g / t[:, None]),
            "hyper_graph": bf(np.random.uniform(size=(B, N, E)) * (t * t)[:, None] * u),
            "W_line": bf((1.0 + 0.1 * np.random.standard_normal(E)) * sign / u)}


def reference(node_features, hyper_graph, W_line):
    X = f64(node_features)
    H = f64(hyper_graph)
    w_abs = np.abs(f64(W_line))
    b_deg = np.sum(H, axis=-2)
    d_deg = np.sum(H * w_abs, axis=-1)
    d_inv = d_deg ** -0.5
    d_inv = np.where(np.isinf(d_inv), 0.0, d_inv)
    b_inv = 1.0 / b_deg
    b_inv = np.where(np.isinf(b_inv), 0.0, b_inv)
    Xs = X * d_inv[..., :, None]
    tmp = mxq(H, 1, "e4m3").transpose(0, 2, 1) @ mxq(Xs, 1, "e4m3")
    tmp = tmp * (w_abs[None, :, None] * b_inv[:, :, None])
    Hs = H * d_inv[..., :, None]
    return mxq(Hs, 2, "e4m3") @ mxq(tmp, 1, "e4m3")

@@ -1,0 +1,230 @@
+from contextlib import ExitStack
+
+import concourse.mybir as mybir
+from concourse.masks import make_identity
+
+FP8X4 = mybir.dt.float8_e4m3fn_x4
+BF16 = mybir.dt.bfloat16
+F32 = mybir.dt.float32
+U32 = mybir.dt.uint32
+U8 = mybir.dt.uint8
+ALU = mybir.AluOpType
+
+B, N, E, F = 4, 1024, 1024, 128
+P = 128
+PACK = 4
+NPASS = 2
+NT = 8
+
+FLOPS = 2 * 2 * B * N * E * F
+
+
+def tile_hgcn_t_kernel(tc, node_features, hyper_graph, W_line, out):
+    nc = tc.nc
+    with ExitStack() as ctx:
+        const = ctx.enter_context(tc.tile_pool(name="const", bufs=1))
+        rawp = ctx.enter_context(tc.tile_pool(name="rawp", bufs=1))
+        htp = ctx.enter_context(tc.tile_pool(name="htp", bufs=3))
+        hsp = ctx.enter_context(tc.tile_pool(name="hsp", bufs=3))
+        g1p = ctx.enter_context(tc.tile_pool(name="g1p", bufs=2))
+        g2p = ctx.enter_context(tc.tile_pool(name="g2p", bufs=2))
+        qp = ctx.enter_context(tc.tile_pool(name="qp", bufs=2))
+        small = ctx.enter_context(tc.tile_pool(name="small", bufs=3))
+        xp = ctx.enter_context(tc.tile_pool(name="xp", bufs=2))
+        op = ctx.enter_context(tc.tile_pool(name="op", bufs=4))
+        psum = ctx.enter_context(tc.psum_pool(name="psum", bufs=1))
+
+        ident = const.tile([P, P], BF16)
+        make_identity(nc, ident[:])
+        ones = const.tile([P, 1], BF16)
+        nc.vector.memset(ones[:], 1.0)
+        wrows = const.tile([P, P], BF16)
+        nc.vector.memset(wrows[:], 0.0)
+        nc.sync.dma_start(out=wrows[0:NT, :], in_=W_line.rearrange("(s m) -> s m", m=P))
+
+        raw = {}
+        xraw = {}
+        for b in range(B):
+            for c in range(NPASS):
+                raw[(b, c)] = rawp.tile([P, PACK, E], BF16, name="raw%d%d" % (b, c))
+                nc.sync.dma_start(
+                    out=raw[(b, c)][:],
+                    in_=hyper_graph[b, c * 512 : (c + 1) * 512, :].rearrange("(p j) e -> p j e", j=PACK),
+                )
+            xraw[b] = rawp.tile([P, NPASS, PACK, F], BF16, name="xraw%d" % b)
+            nc.sync.dma_start(
+                out=xraw[b][:],
+                in_=node_features[b].rearrange("(c p j) f -> p c j f", c=NPASS, j=PACK),
+            )
+
+        wt_ps = psum.tile([P, NT, P], BF16, tag="tp", bufs=4)
+        nc.tensor.transpose(wt_ps[:, 0, :], wrows[:], ident[:])
+        wsb = const.tile([P, NT], F32)
+        nc.vector.tensor_copy(out=wsb[:], in_=wt_ps[:, 0, 0:NT])
+        wabs_f = const.tile([P, NT], F32)
+        nc.vector.scalar_tensor_tensor(
+            out=wabs_f[:], in0=wsb[:], scalar=-1.0, in1=wsb[:], op0=ALU.mult, op1=ALU.max
+        )
+        wabs_b = const.tile([P, NT], BF16)
+        nc.vector.tensor_copy(out=wabs_b[:], in_=wabs_f[:])
+
+        state = {}
+
+        def safe_inverse(src_ps, root, nm):
+            x = small.tile([P, NT], F32, name=nm + "_x")
+            nc.vector.tensor_copy(out=x[:], in_=src_ps[:])
+            nz = small.tile([P, NT], F32, name=nm + "_nz")
+            nc.vector.scalar_tensor_tensor(
+                out=nz[:], in0=x[:], scalar=0.0, in1=x[:], op0=ALU.is_equal, op1=ALU.add
+            )
+            if root:
+                sq = small.tile([P, NT], F32, name=nm + "_sq")
+                nc.scalar.sqrt(out=sq[:], in_=nz[:])
+                nz = sq
+            rc = small.tile([P, NT], F32, name=nm + "_rc")
+            nc.vector.reciprocal(out=rc[:], in_=nz[:])
+            res = small.tile([P, NT], F32, name=nm + "_inv")
+            nc.vector.scalar_tensor_tensor(
+                out=res[:], in0=x[:], scalar=0.0, in1=rc[:], op0=ALU.not_equal, op1=ALU.mult
+            )
+            return res
+
+        def stage_a(b):
+            codes1 = qp.tile([P, NPASS, E], U32, name="codes1", align_bytes=64)
+            scales1 = qp.tile([P, NPASS, E], U8, name="scales1", align_bytes=64)
+            hts = []
+            for c in range(NPASS):
+                r = raw[(b, c)]
+                ht = htp.tile([P, PACK, NT, P], BF16, name="ht")
+                hts.append(ht)
+                for j in range(PACK):
+                    tp = psum.tile([P, NT, P], BF16, tag="tp", bufs=4, name="tp1")
+                    for s in range(NT):
+                        nc.tensor.transpose(tp[:, s, :], r[:, j, s * P : (s + 1) * P], ident[:])
+                    nc.scalar.copy(
+                        out=ht[:, j, :, :].rearrange("m s p -> m (s p)").bitcast(F32),
+                        in_=tp[:].rearrange("m s p -> m (s p)").bitcast(F32),
+                    )
+                g1 = g1p.tile([P, E, PACK], BF16, name="g1", align_bytes=64)
+                nc.vector.tensor_copy(
+                    out=g1[:].rearrange("p (c i) t -> p c t i", i=4),
+                    in_=r[:].rearrange("p t (c i) -> p c t i", i=4),
+                )
+                nc.vector.quantize_mx(
+                    out=codes1[:, c, :].bitcast(FP8X4),
+                    scales=scales1[:, c, :],
+                    in_=g1[:].rearrange("p e j -> p (e j)"),
+                )
+            bd = psum.tile([P, NT], F32, tag="deg", bufs=2, name="bd")
+            for s in range(NT):
+                for cj in range(NT):
+                    nc.tensor.matmul(
+                        bd[:, s : s + 1],
+                        lhsT=raw[(b, cj // PACK)][:, cj % PACK, s * P : (s + 1) * P],
+                        rhs=ones[:],
+                        start=(cj == 0),
+                        stop=(cj == NT - 1),
+                    )
+            dd = psum.tile([P, NT], F32, tag="deg", bufs=2, name="dd")
+            for cj in range(NT):
+                for s in range(NT):
+                    nc.tensor.matmul(
+                        dd[:, cj : cj + 1],
+                        lhsT=hts[cj // PACK][:, cj % PACK, s, :],
+                        rhs=wabs_b[:, s : s + 1],
+                        start=(s == 0),
+                        stop=(s == NT - 1),
+                    )
+            dinv = safe_inverse(dd, True, "d")
+            binv = safe_inverse(bd, False, "b")
+            wb = small.tile([P, NT], F32, name="wb")
+            nc.vector.tensor_tensor(out=wb[:], in0=binv[:], in1=wabs_f[:], op=ALU.mult)
+            state[b] = (codes1, scales1, dinv, wb)
+
+        def stage_c(b):
+            codes1, scales1, dinv, wb = state[b]
+            xg = xp.tile([P, NPASS, F, PACK], BF16, name="xg", align_bytes=64)
+            for c in range(NPASS):
+                nc.vector.tensor_tensor(
+                    out=xg[:, c, :, :],
+                    in0=xraw[b][:, c, :, :].rearrange("p j f -> p f j"),
+                    in1=dinv[:, c * PACK : (c + 1) * PACK].unsqueeze(1).to_broadcast([P, F, PACK]),
+                    op=ALU.mult,
+                )
+            xq = xp.tile([P, NPASS * F], U32, name="xq", align_bytes=64)
+            xs = xp.tile([P, NPASS * F], U8, name="xs", align_bytes=64)
+            nc.vector.quantize_mx(
+                out=xq[:].bitcast(FP8X4), scales=xs[:], in_=xg[:].rearrange("p c f j -> p (c f j)")
+            )
+            t2g = xp.tile([P, NPASS, F, PACK], BF16, name="t2g", align_bytes=64)
+            for g in range(NPASS):
+                tmp_ps = psum.tile([P, PACK, F], F32, tag="mm1", bufs=1, name="tmp_ps")
+                for t in range(PACK):
+                    s = g * PACK + t
+                    for c in range(NPASS):
+                        nc.tensor.matmul_mx(
+                            out=tmp_ps[:, t, :],
+                            lhsT=codes1[:, c, s * P : (s + 1) * P].bitcast(FP8X4),
+                            lhsT_scale=scales1[:, c, s * P : (s + 1) * P],
+                            rhs=xq[:, c * F : (c + 1) * F].bitcast(FP8X4),
+                            rhs_scale=xs[:, c * F : (c + 1) * F],
+                            start=(c == 0),
+                            stop=(c == NPASS - 1),
+                        )
+                nc.vector.tensor_tensor(
+                    out=t2g[:, g, :, :],
+                    in0=tmp_ps[:].rearrange("m t f -> m f t"),
+                    in1=wb[:, g * PACK : (g + 1) * PACK].unsqueeze(1).to_broadcast([P, F, PACK]),
+                    op=ALU.mult,
+                )
+            t2q = xp.tile([P, NPASS * F], U32, name="t2q", align_bytes=64)
+            t2s = xp.tile([P, NPASS * F], U8, name="t2s", align_bytes=64)
+            nc.vector.quantize_mx(
+                out=t2q[:].bitcast(FP8X4), scales=t2s[:], in_=t2g[:].rearrange("p g f t -> p (g f t)")
+            )
+            for c in range(NPASS):
+                r = raw[(b, c)]
+                hs = hsp.tile([P, PACK, E], BF16, name="hs")
+                g2 = g2p.tile([P, PACK, NPASS, P, PACK], BF16, name="g2", align_bytes=64)
+                for j in range(PACK):
+                    cj = c * PACK + j
+                    nc.vector.tensor_scalar(
+                        out=hs[:, j, :], in0=r[:, j, :], scalar1=dinv[:, cj : cj + 1], scalar2=None, op0=ALU.mult
+                    )
+                    tp = psum.tile([P, NT, P], BF16, tag="tp", bufs=4, name="tp2")
+                    for s in range(NT):
+                        nc.tensor.transpose(tp[:, s, :], hs[:, j, s * P : (s + 1) * P], ident[:])
+                    nc.scalar.copy(
+                        out=g2[:, j, :, :, :], in_=tp[:].rearrange("m (g t) p -> m g p t", t=PACK)
+                    )
+                codes2 = qp.tile([P, PACK * NPASS * P], U32, name="codes2", align_bytes=64)
+                scales2 = qp.tile([P, PACK * NPASS * P], U8, name="scales2", align_bytes=64)
+                nc.vector.quantize_mx(
+                    out=codes2[:].bitcast(FP8X4),
+                    scales=scales2[:],
+                    in_=g2[:].rearrange("m j g p t -> m (j g p t)"),
+                )
+                o_ps = psum.tile([P, PACK, F], F32, tag="mm2", bufs=1, name="o_ps")
+                for j in range(PACK):
+                    for g in range(NPASS):
+                        k = (j * NPASS + g) * P
+                        nc.tensor.matmul_mx(
+                            out=o_ps[:, j, :],
+                            lhsT=codes2[:, k : k + P].bitcast(FP8X4),
+                            lhsT_scale=scales2[:, k : k + P],
+                            rhs=t2q[:, g * F : (g + 1) * F].bitcast(FP8X4),
+                            rhs_scale=t2s[:, g * F : (g + 1) * F],
+                            start=(g == 0),
+                            stop=(g == NPASS - 1),
+                        )
+                osb = op.tile([P, PACK, F], F32, name="osb")
+                nc.scalar.copy(out=osb[:], in_=o_ps[:])
+                nc.sync.dma_start(
+                    out=out[b, c * 512 : (c + 1) * 512, :].rearrange("(p j) f -> p j f", j=PACK), in_=osb[:]
+                )
+
+        stage_a(0)
+        for b in range(1, B):
+            stage_a(b)
+            stage_c(b - 1)
+        stage_c(B - 1)

@@ -13,30 +13,113 @@ ALU = mybir.AluOpType
 B, N, E, F = 4, 1024, 1024, 128
 P = 128
 PACK = 4
-NPASS = 2
 NT = 8
+NHALF = 8
+NTILE = 32
+ND = 12
+LEAD = 8
+SC_AHEAD = 2
+M1_LAG = 2
+NWARM = 6
+TINY = 2.0 ** -100
 
 FLOPS = 2 * 2 * B * N * E * F
+
+
+def schedule():
+    ops = []
+    add = ops.append
+
+    def step_of_cda(h):
+        return 4 * h + 4 - LEAD
+
+    m1s = [max(step_of_cda(2 * b + 1) + M1_LAG, 0) for b in range(B)]
+    m2s = {}
+    for b in range(B):
+        m2s[2 * b] = max(m1s[b] + 5, 8 * b + 5)
+        m2s[2 * b + 1] = max(m2s[2 * b] + 2, 8 * b + 9)
+    last = max(m2s.values()) + 3
+    for sg in range(-LEAD, last):
+        t1_tile = sg + LEAD
+        for h in range(NHALF):
+            if sg == step_of_cda(h) + 1:
+                add(("cdb", h))
+                add(("xs", h))
+                if h % 2 == 1:
+                    add(("qx", h // 2))
+        for b in range(B):
+            if sg == m1s[b] + 2:
+                add(("tm", b, 0))
+            if sg == m1s[b] + 4:
+                add(("tm", b, 1))
+                add(("qt", b))
+        for tau in range(NTILE):
+            if max(tau - SC_AHEAD, step_of_cda(tau // 4) + 1) == sg:
+                add(("sc", tau))
+        if sg % 4 == 0 and 4 <= sg < NTILE:
+            add(("q2", sg // 4 - 1, -1))
+        h, r = t1_tile // 4, t1_tile % 4
+        if 0 <= h < NHALF:
+            if r == 1:
+                add(("r1", h, 0))
+            elif r == 2:
+                add(("r1", h, 1))
+            elif r == 3:
+                add(("q1", h))
+        for b in range(B):
+            if sg == m1s[b]:
+                add(("cb", b))
+        if 0 <= sg < NTILE:
+            add(("t2", sg))
+            if sg >= NTILE - 4:
+                add(("q2", NHALF - 1, sg % 4))
+        if 0 <= t1_tile < NTILE:
+            add(("t1", t1_tile))
+        if 0 <= t1_tile - 1 < NTILE:
+            add(("dmm", t1_tile - 1))
+        for h in range(NHALF):
+            if sg == step_of_cda(h):
+                add(("cda", h))
+                add(("cds", h))
+        for b in range(B):
+            if m1s[b] <= sg < m1s[b] + 4:
+                add(("m1", b, 2 * (sg - m1s[b])))
+                add(("m1", b, 2 * (sg - m1s[b]) + 1))
+        for h in range(NHALF):
+            if m2s[h] <= sg < m2s[h] + 2:
+                add(("m2", 4 * h + 2 * (sg - m2s[h])))
+                add(("m2", 4 * h + 2 * (sg - m2s[h]) + 1))
+            if sg == m2s[h] + 1:
+                add(("eo", h))
+        if 0 <= t1_tile < NTILE:
+            add(("bmm", t1_tile // 4, t1_tile % 4))
+    return ops
 
 
 def tile_hgcn_t_kernel(tc, node_features, hyper_graph, W_line, out):
     nc = tc.nc
     with ExitStack() as ctx:
+        ctx.enter_context(tc.manual_schedule())
         const = ctx.enter_context(tc.tile_pool(name="const", bufs=1))
         rawp = ctx.enter_context(tc.tile_pool(name="rawp", bufs=1))
-        htp = ctx.enter_context(tc.tile_pool(name="htp", bufs=3))
-        hsp = ctx.enter_context(tc.tile_pool(name="hsp", bufs=3))
+        htp = ctx.enter_context(tc.tile_pool(name="htp", bufs=2))
+        hsp = ctx.enter_context(tc.tile_pool(name="hsp", bufs=2))
         g1p = ctx.enter_context(tc.tile_pool(name="g1p", bufs=2))
         g2p = ctx.enter_context(tc.tile_pool(name="g2p", bufs=2))
         qp = ctx.enter_context(tc.tile_pool(name="qp", bufs=2))
-        small = ctx.enter_context(tc.tile_pool(name="small", bufs=3))
+        small = ctx.enter_context(tc.tile_pool(name="small", bufs=4))
         xp = ctx.enter_context(tc.tile_pool(name="xp", bufs=2))
-        op = ctx.enter_context(tc.tile_pool(name="op", bufs=4))
+        op = ctx.enter_context(tc.tile_pool(name="op", bufs=3))
         psum = ctx.enter_context(tc.psum_pool(name="psum", bufs=1))
 
         ident = const.tile([P, P], BF16)
         make_identity(nc, ident[:])
-        ones = const.tile([P, 1], BF16)
+        wzb = const.tile([P, 2048], BF16, align_bytes=64)
+        nc.vector.memset(wzb[:], 0.0)
+        wz = const.tile([P, 512], U32, align_bytes=64)
+        wzs = const.tile([P, 512], U8, align_bytes=64)
+        nc.vector.quantize_mx(out=wz[:].bitcast(FP8X4), scales=wzs[:], in_=wzb[:])
+        ones = const.tile([P, ND], BF16)
         nc.vector.memset(ones[:], 1.0)
         wrows = const.tile([P, P], BF16)
         nc.vector.memset(wrows[:], 0.0)
@@ -44,20 +127,34 @@ def tile_hgcn_t_kernel(tc, node_features, hyper_graph, W_line, out):
 
         raw = {}
         xraw = {}
-        for b in range(B):
-            for c in range(NPASS):
-                raw[(b, c)] = rawp.tile([P, PACK, E], BF16, name="raw%d%d" % (b, c))
+        for h in range(NHALF):
+            b, c = h // 2, h % 2
+            raw[h] = rawp.tile([P, PACK, E], BF16, name="raw%d" % h)
+            src = hyper_graph[b, c * 512 : (c + 1) * 512, :].rearrange("(p j) e -> p j e", j=PACK)
+            if h == 0:
+                for j in range(PACK):
+                    nc.sync.dma_start(out=raw[h][:, j, :], in_=src[:, j, :])
+            else:
+                nc.sync.dma_start(out=raw[h][:], in_=src)
+            if c == 1:
+                xraw[b] = rawp.tile([P, 2, PACK, F], BF16, name="xraw%d" % b)
                 nc.sync.dma_start(
-                    out=raw[(b, c)][:],
-                    in_=hyper_graph[b, c * 512 : (c + 1) * 512, :].rearrange("(p j) e -> p j e", j=PACK),
+                    out=xraw[b][:], in_=node_features[b].rearrange("(c p j) f -> p c j f", c=2, j=PACK)
                 )
-            xraw[b] = rawp.tile([P, NPASS, PACK, F], BF16, name="xraw%d" % b)
-            nc.sync.dma_start(
-                out=xraw[b][:],
-                in_=node_features[b].rearrange("(c p j) f -> p c j f", c=NPASS, j=PACK),
+
+        warm_ps = psum.tile([P, 512], F32, tag="mm", bufs=2, name="warm_ps")
+        for i in range(NWARM):
+            nc.tensor.matmul_mx(
+                out=warm_ps[:],
+                lhsT=wz[:, 0:P].bitcast(FP8X4),
+                lhsT_scale=wzs[:, 0:P],
+                rhs=wz[:].bitcast(FP8X4),
+                rhs_scale=wzs[:],
+                start=True,
+                stop=True,
             )
 
-        wt_ps = psum.tile([P, NT, P], BF16, tag="tp", bufs=4)
+        wt_ps = psum.tile([P, PACK, P], BF16, tag="tp", bufs=4, name="wt_ps")
         nc.tensor.transpose(wt_ps[:, 0, :], wrows[:], ident[:])
         wsb = const.tile([P, NT], F32)
         nc.vector.tensor_copy(out=wsb[:], in_=wt_ps[:, 0, 0:NT])
@@ -65,166 +162,232 @@ def tile_hgcn_t_kernel(tc, node_features, hyper_graph, W_line, out):
         nc.vector.scalar_tensor_tensor(
             out=wabs_f[:], in0=wsb[:], scalar=-1.0, in1=wsb[:], op0=ALU.mult, op1=ALU.max
         )
-        wabs_b = const.tile([P, NT], BF16)
-        nc.vector.tensor_copy(out=wabs_b[:], in_=wabs_f[:])
+        wrep = const.tile([P, NT, ND], BF16)
+        nc.vector.tensor_copy(out=wrep[:], in_=wabs_f[:].unsqueeze(2).to_broadcast([P, NT, ND]))
 
-        state = {}
+        st = {}
 
-        def safe_inverse(src_ps, root, nm):
-            x = small.tile([P, NT], F32, name=nm + "_x")
-            nc.vector.tensor_copy(out=x[:], in_=src_ps[:])
-            nz = small.tile([P, NT], F32, name=nm + "_nz")
-            nc.vector.scalar_tensor_tensor(
-                out=nz[:], in0=x[:], scalar=0.0, in1=x[:], op0=ALU.is_equal, op1=ALU.add
-            )
-            if root:
-                sq = small.tile([P, NT], F32, name=nm + "_sq")
-                nc.scalar.sqrt(out=sq[:], in_=nz[:])
-                nz = sq
-            rc = small.tile([P, NT], F32, name=nm + "_rc")
-            nc.vector.reciprocal(out=rc[:], in_=nz[:])
-            res = small.tile([P, NT], F32, name=nm + "_inv")
-            nc.vector.scalar_tensor_tensor(
-                out=res[:], in0=x[:], scalar=0.0, in1=rc[:], op0=ALU.not_equal, op1=ALU.mult
-            )
-            return res
+        def transposes(src_tile, j, g, nm):
+            tp = psum.tile([P, PACK, P], BF16, tag="tp", bufs=4, name=nm)
+            for t in range(PACK):
+                s = g * PACK + t
+                nc.tensor.transpose(tp[:, t, :], src_tile[:, j, s * P : (s + 1) * P], ident[:])
+            return tp
 
-        def stage_a(b):
-            codes1 = qp.tile([P, NPASS, E], U32, name="codes1", align_bytes=64)
-            scales1 = qp.tile([P, NPASS, E], U8, name="scales1", align_bytes=64)
-            hts = []
-            for c in range(NPASS):
-                r = raw[(b, c)]
-                ht = htp.tile([P, PACK, NT, P], BF16, name="ht")
-                hts.append(ht)
-                for j in range(PACK):
-                    tp = psum.tile([P, NT, P], BF16, tag="tp", bufs=4, name="tp1")
-                    for s in range(NT):
-                        nc.tensor.transpose(tp[:, s, :], r[:, j, s * P : (s + 1) * P], ident[:])
+        for o in schedule():
+            k = o[0]
+            if k == "t1":
+                h, j = o[1] // 4, o[1] % 4
+                if j == 0:
+                    st[("ht", h)] = htp.tile([P, PACK, NT, P], BF16, name="ht")
+                ht = st[("ht", h)]
+                for g in range(2):
+                    tp = transposes(raw[h], j, g, "tp1")
                     nc.scalar.copy(
-                        out=ht[:, j, :, :].rearrange("m s p -> m (s p)").bitcast(F32),
+                        out=ht[:, j, g * PACK : (g + 1) * PACK, :].rearrange("m s p -> m (s p)").bitcast(F32),
                         in_=tp[:].rearrange("m s p -> m (s p)").bitcast(F32),
                     )
-                g1 = g1p.tile([P, E, PACK], BF16, name="g1", align_bytes=64)
-                nc.vector.tensor_copy(
-                    out=g1[:].rearrange("p (c i) t -> p c t i", i=4),
-                    in_=r[:].rearrange("p t (c i) -> p c t i", i=4),
+            elif k == "bmm":
+                h, r = o[1], o[2]
+                if r == 0:
+                    st[("deg", h)] = psum.tile([P, PACK + NT, ND], F32, tag="deg", bufs=2, name="deg")
+                deg = st[("deg", h)]
+                for s in (2 * r, 2 * r + 1):
+                    for j in range(PACK):
+                        nc.tensor.matmul(
+                            deg[:, PACK + s, :],
+                            lhsT=raw[h][:, j, s * P : (s + 1) * P],
+                            rhs=ones[:],
+                            start=(j == 0),
+                            stop=(j == PACK - 1),
+                        )
+            elif k == "dmm":
+                h, j = o[1] // 4, o[1] % 4
+                deg = st[("deg", h)]
+                ht = st[("ht", h)]
+                for s in range(NT):
+                    nc.tensor.matmul(
+                        deg[:, j, :], lhsT=ht[:, j, s, :], rhs=wrep[:, s, :], start=(s == 0), stop=(s == NT - 1)
+                    )
+            elif k == "cda":
+                h = o[1]
+                nz = small.tile([P, PACK], F32, name="d_nz")
+                nc.vector.tensor_scalar(
+                    out=nz[:], in0=st[("deg", h)][:, 0:PACK, 0], scalar1=TINY, scalar2=None, op0=ALU.max
                 )
+                st[("nz", h)] = nz
+            elif k == "cds":
+                h = o[1]
+                sq = small.tile([P, PACK], F32, name="d_sq")
+                nc.scalar.sqrt(out=sq[:], in_=st[("nz", h)][:])
+                st[("sq", h)] = sq
+                bsb = small.tile([P, NT], F32, name="b_part")
+                nc.scalar.copy(out=bsb[:], in_=st[("deg", h)][:, PACK : PACK + NT, 0])
+                st[("bsb", h)] = bsb
+            elif k == "cdb":
+                h = o[1]
+                rc = small.tile([P, PACK], F32, name="d_rc")
+                nc.vector.reciprocal(out=rc[:], in_=st[("sq", h)][:])
+                dinv = small.tile([P, PACK], F32, name="d_inv")
+                nc.vector.scalar_tensor_tensor(
+                    out=dinv[:], in0=st[("deg", h)][:, 0:PACK, 0], scalar=0.0, in1=rc[:], op0=ALU.is_gt, op1=ALU.mult
+                )
+                st[("dinv", h)] = dinv
+            elif k == "cb":
+                b = o[1]
+                bs = small.tile([P, NT], F32, name="b_sum")
+                nc.vector.tensor_tensor(
+                    out=bs[:], in0=st[("bsb", 2 * b)][:], in1=st[("bsb", 2 * b + 1)][:], op=ALU.add
+                )
+                bnz = small.tile([P, NT], F32, name="b_nz")
+                nc.vector.scalar_tensor_tensor(
+                    out=bnz[:], in0=bs[:], scalar=0.0, in1=bs[:], op0=ALU.is_equal, op1=ALU.add
+                )
+                brc = small.tile([P, NT], F32, name="b_rc")
+                nc.vector.reciprocal(out=brc[:], in_=bnz[:])
+                binv = small.tile([P, NT], F32, name="b_inv")
+                nc.vector.scalar_tensor_tensor(
+                    out=binv[:], in0=bs[:], scalar=0.0, in1=brc[:], op0=ALU.not_equal, op1=ALU.mult
+                )
+                wb = small.tile([P, NT], F32, name="wb")
+                nc.vector.tensor_tensor(out=wb[:], in0=binv[:], in1=wabs_f[:], op=ALU.mult)
+                st[("wb", b)] = wb
+            elif k == "xs":
+                h = o[1]
+                b, c = h // 2, h % 2
+                if c == 0:
+                    st[("xg", b)] = xp.tile([P, 2, F, PACK], BF16, name="xg", align_bytes=64)
+                nc.vector.tensor_tensor(
+                    out=st[("xg", b)][:, c, :, :],
+                    in0=xraw[b][:, c, :, :].rearrange("p j f -> p f j"),
+                    in1=st[("dinv", h)][:].unsqueeze(1).to_broadcast([P, F, PACK]),
+                    op=ALU.mult,
+                )
+            elif k == "qx":
+                b = o[1]
+                xq = xp.tile([P, 2 * F], U32, name="xq", align_bytes=64)
+                xs = xp.tile([P, 2 * F], U8, name="xs", align_bytes=64)
+                nc.vector.quantize_mx(
+                    out=xq[:].bitcast(FP8X4), scales=xs[:], in_=st[("xg", b)][:].rearrange("p c f j -> p (c f j)")
+                )
+                st[("xq", b)] = (xq, xs)
+            elif k == "sc":
+                h, j = o[1] // 4, o[1] % 4
+                if j == 0:
+                    st[("hs", h)] = hsp.tile([P, PACK, E], BF16, name="hs")
+                nc.vector.tensor_scalar(
+                    out=st[("hs", h)][:, j, :],
+                    in0=raw[h][:, j, :],
+                    scalar1=st[("dinv", h)][:, j : j + 1],
+                    scalar2=None,
+                    op0=ALU.mult,
+                )
+            elif k == "t2":
+                h, j = o[1] // 4, o[1] % 4
+                if j == 0:
+                    st[("g2", h)] = g2p.tile([P, PACK, 2, P, PACK], BF16, name="g2", align_bytes=64)
+                for g in range(2):
+                    tp = transposes(st[("hs", h)], j, g, "tp2")
+                    nc.scalar.copy(out=st[("g2", h)][:, j, g, :, :], in_=tp[:].rearrange("m t p -> m p t"))
+            elif k == "q2":
+                h, j = o[1], o[2]
+                if j <= 0:
+                    codes2 = qp.tile([P, PACK * 2 * P], U32, name="codes2", align_bytes=64)
+                    scales2 = qp.tile([P, PACK * 2 * P], U8, name="scales2", align_bytes=64)
+                    st[("q2", h)] = (codes2, scales2)
+                codes2, scales2 = st[("q2", h)]
+                if j < 0:
+                    nc.vector.quantize_mx(
+                        out=codes2[:].bitcast(FP8X4),
+                        scales=scales2[:],
+                        in_=st[("g2", h)][:].rearrange("m j g p t -> m (j g p t)"),
+                    )
+                else:
+                    w = 2 * P
+                    nc.vector.quantize_mx(
+                        out=codes2[:, j * w : (j + 1) * w].bitcast(FP8X4),
+                        scales=scales2[:, j * w : (j + 1) * w],
+                        in_=st[("g2", h)][:, j, :, :, :].rearrange("m g p t -> m (g p t)"),
+                    )
+            elif k == "r1":
+                h, x = o[1], o[2]
+                if x == 0:
+                    st[("g1", h)] = g1p.tile([P, E, PACK], BF16, name="g1", align_bytes=64)
+                e0, e1 = x * 512, (x + 1) * 512
+                nc.vector.tensor_copy(
+                    out=st[("g1", h)][:, e0:e1, :].rearrange("p (c i) t -> p c t i", i=4),
+                    in_=raw[h][:, :, e0:e1].rearrange("p t (c i) -> p c t i", i=4),
+                )
+            elif k == "q1":
+                h = o[1]
+                b, c = h // 2, h % 2
+                if c == 0:
+                    codes1 = qp.tile([P, 2, E], U32, name="codes1", align_bytes=64)
+                    scales1 = qp.tile([P, 2, E], U8, name="scales1", align_bytes=64)
+                    st[("q1", b)] = (codes1, scales1)
+                codes1, scales1 = st[("q1", b)]
                 nc.vector.quantize_mx(
                     out=codes1[:, c, :].bitcast(FP8X4),
                     scales=scales1[:, c, :],
-                    in_=g1[:].rearrange("p e j -> p (e j)"),
+                    in_=st[("g1", h)][:].rearrange("p e j -> p (e j)"),
                 )
-            bd = psum.tile([P, NT], F32, tag="deg", bufs=2, name="bd")
-            for s in range(NT):
-                for cj in range(NT):
-                    nc.tensor.matmul(
-                        bd[:, s : s + 1],
-                        lhsT=raw[(b, cj // PACK)][:, cj % PACK, s * P : (s + 1) * P],
-                        rhs=ones[:],
-                        start=(cj == 0),
-                        stop=(cj == NT - 1),
+            elif k == "m1":
+                b, s = o[1], o[2]
+                g, t = s // PACK, s % PACK
+                if t == 0:
+                    st[("tmp", b, g)] = psum.tile([P, PACK, F], F32, tag="mm", bufs=2, name="tmp_ps")
+                codes1, scales1 = st[("q1", b)]
+                xq, xs = st[("xq", b)]
+                for c in range(2):
+                    nc.tensor.matmul_mx(
+                        out=st[("tmp", b, g)][:, t, :],
+                        lhsT=codes1[:, c, s * P : (s + 1) * P].bitcast(FP8X4),
+                        lhsT_scale=scales1[:, c, s * P : (s + 1) * P],
+                        rhs=xq[:, c * F : (c + 1) * F].bitcast(FP8X4),
+                        rhs_scale=xs[:, c * F : (c + 1) * F],
+                        start=(c == 0),
+                        stop=(c == 1),
                     )
-            dd = psum.tile([P, NT], F32, tag="deg", bufs=2, name="dd")
-            for cj in range(NT):
-                for s in range(NT):
-                    nc.tensor.matmul(
-                        dd[:, cj : cj + 1],
-                        lhsT=hts[cj // PACK][:, cj % PACK, s, :],
-                        rhs=wabs_b[:, s : s + 1],
-                        start=(s == 0),
-                        stop=(s == NT - 1),
-                    )
-            dinv = safe_inverse(dd, True, "d")
-            binv = safe_inverse(bd, False, "b")
-            wb = small.tile([P, NT], F32, name="wb")
-            nc.vector.tensor_tensor(out=wb[:], in0=binv[:], in1=wabs_f[:], op=ALU.mult)
-            state[b] = (codes1, scales1, dinv, wb)
-
-        def stage_c(b):
-            codes1, scales1, dinv, wb = state[b]
-            xg = xp.tile([P, NPASS, F, PACK], BF16, name="xg", align_bytes=64)
-            for c in range(NPASS):
+            elif k == "tm":
+                b, g = o[1], o[2]
+                if g == 0:
+                    st[("t2g", b)] = xp.tile([P, 2, F, PACK], BF16, name="t2g", align_bytes=64)
                 nc.vector.tensor_tensor(
-                    out=xg[:, c, :, :],
-                    in0=xraw[b][:, c, :, :].rearrange("p j f -> p f j"),
-                    in1=dinv[:, c * PACK : (c + 1) * PACK].unsqueeze(1).to_broadcast([P, F, PACK]),
+                    out=st[("t2g", b)][:, g, :, :],
+                    in0=st[("tmp", b, g)][:].rearrange("m t f -> m f t"),
+                    in1=st[("wb", b)][:, g * PACK : (g + 1) * PACK].unsqueeze(1).to_broadcast([P, F, PACK]),
                     op=ALU.mult,
                 )
-            xq = xp.tile([P, NPASS * F], U32, name="xq", align_bytes=64)
-            xs = xp.tile([P, NPASS * F], U8, name="xs", align_bytes=64)
-            nc.vector.quantize_mx(
-                out=xq[:].bitcast(FP8X4), scales=xs[:], in_=xg[:].rearrange("p c f j -> p (c f j)")
-            )
-            t2g = xp.tile([P, NPASS, F, PACK], BF16, name="t2g", align_bytes=64)
-            for g in range(NPASS):
-                tmp_ps = psum.tile([P, PACK, F], F32, tag="mm1", bufs=1, name="tmp_ps")
-                for t in range(PACK):
-                    s = g * PACK + t
-                    for c in range(NPASS):
-                        nc.tensor.matmul_mx(
-                            out=tmp_ps[:, t, :],
-                            lhsT=codes1[:, c, s * P : (s + 1) * P].bitcast(FP8X4),
-                            lhsT_scale=scales1[:, c, s * P : (s + 1) * P],
-                            rhs=xq[:, c * F : (c + 1) * F].bitcast(FP8X4),
-                            rhs_scale=xs[:, c * F : (c + 1) * F],
-                            start=(c == 0),
-                            stop=(c == NPASS - 1),
-                        )
-                nc.vector.tensor_tensor(
-                    out=t2g[:, g, :, :],
-                    in0=tmp_ps[:].rearrange("m t f -> m f t"),
-                    in1=wb[:, g * PACK : (g + 1) * PACK].unsqueeze(1).to_broadcast([P, F, PACK]),
-                    op=ALU.mult,
-                )
-            t2q = xp.tile([P, NPASS * F], U32, name="t2q", align_bytes=64)
-            t2s = xp.tile([P, NPASS * F], U8, name="t2s", align_bytes=64)
-            nc.vector.quantize_mx(
-                out=t2q[:].bitcast(FP8X4), scales=t2s[:], in_=t2g[:].rearrange("p g f t -> p (g f t)")
-            )
-            for c in range(NPASS):
-                r = raw[(b, c)]
-                hs = hsp.tile([P, PACK, E], BF16, name="hs")
-                g2 = g2p.tile([P, PACK, NPASS, P, PACK], BF16, name="g2", align_bytes=64)
-                for j in range(PACK):
-                    cj = c * PACK + j
-                    nc.vector.tensor_scalar(
-                        out=hs[:, j, :], in0=r[:, j, :], scalar1=dinv[:, cj : cj + 1], scalar2=None, op0=ALU.mult
-                    )
-                    tp = psum.tile([P, NT, P], BF16, tag="tp", bufs=4, name="tp2")
-                    for s in range(NT):
-                        nc.tensor.transpose(tp[:, s, :], hs[:, j, s * P : (s + 1) * P], ident[:])
-                    nc.scalar.copy(
-                        out=g2[:, j, :, :, :], in_=tp[:].rearrange("m (g t) p -> m g p t", t=PACK)
-                    )
-                codes2 = qp.tile([P, PACK * NPASS * P], U32, name="codes2", align_bytes=64)
-                scales2 = qp.tile([P, PACK * NPASS * P], U8, name="scales2", align_bytes=64)
+            elif k == "qt":
+                b = o[1]
+                t2q = xp.tile([P, 2 * F], U32, name="t2q", align_bytes=64)
+                t2s = xp.tile([P, 2 * F], U8, name="t2s", align_bytes=64)
                 nc.vector.quantize_mx(
-                    out=codes2[:].bitcast(FP8X4),
-                    scales=scales2[:],
-                    in_=g2[:].rearrange("m j g p t -> m (j g p t)"),
+                    out=t2q[:].bitcast(FP8X4), scales=t2s[:], in_=st[("t2g", b)][:].rearrange("p g f t -> p (g f t)")
                 )
-                o_ps = psum.tile([P, PACK, F], F32, tag="mm2", bufs=1, name="o_ps")
-                for j in range(PACK):
-                    for g in range(NPASS):
-                        k = (j * NPASS + g) * P
-                        nc.tensor.matmul_mx(
-                            out=o_ps[:, j, :],
-                            lhsT=codes2[:, k : k + P].bitcast(FP8X4),
-                            lhsT_scale=scales2[:, k : k + P],
-                            rhs=t2q[:, g * F : (g + 1) * F].bitcast(FP8X4),
-                            rhs_scale=t2s[:, g * F : (g + 1) * F],
-                            start=(g == 0),
-                            stop=(g == NPASS - 1),
-                        )
+                st[("t2q", b)] = (t2q, t2s)
+            elif k == "m2":
+                h, j = o[1] // 4, o[1] % 4
+                if j == 0:
+                    st[("o", h)] = psum.tile([P, PACK, F], F32, tag="mm", bufs=2, name="o_ps")
+                codes2, scales2 = st[("q2", h)]
+                t2q, t2s = st[("t2q", h // 2)]
+                for g in range(2):
+                    q = (j * 2 + g) * P
+                    nc.tensor.matmul_mx(
+                        out=st[("o", h)][:, j, :],
+                        lhsT=codes2[:, q : q + P].bitcast(FP8X4),
+                        lhsT_scale=scales2[:, q : q + P],
+                        rhs=t2q[:, g * F : (g + 1) * F].bitcast(FP8X4),
+                        rhs_scale=t2s[:, g * F : (g + 1) * F],
+                        start=(g == 0),
+                        stop=(g == 1),
+                    )
+            elif k == "eo":
+                h = o[1]
+                b, c = h // 2, h % 2
                 osb = op.tile([P, PACK, F], F32, name="osb")
-                nc.scalar.copy(out=osb[:], in_=o_ps[:])
+                nc.scalar.copy(out=osb[:], in_=st[("o", h)][:])
                 nc.sync.dma_start(
                     out=out[b, c * 512 : (c + 1) * 512, :].rearrange("(p j) f -> p j f", j=PACK), in_=osb[:]
                 )
-
-        stage_a(0)
-        for b in range(1, B):
-            stage_a(b)
-            stage_c(b - 1)
-        stage_c(B - 1)

@@ -9,6 +9,7 @@ F32 = mybir.dt.float32
 U32 = mybir.dt.uint32
 U8 = mybir.dt.uint8
 ALU = mybir.AluOpType
+ACT = mybir.ActivationFunctionType
 
 B, N, E, F = 4, 1024, 1024, 128
 P = 128
@@ -19,8 +20,9 @@ NTILE = 32
 ND = 12
 LEAD = 8
 SC_AHEAD = 2
-M1_LAG = 2
-NWARM = 6
+M1_LAG = 3
+CDB_LAG = 2
+NWARM = 12
 TINY = 2.0 ** -100
 
 FLOPS = 2 * 2 * B * N * E * F
@@ -42,7 +44,7 @@ def schedule():
     for sg in range(-LEAD, last):
         t1_tile = sg + LEAD
         for h in range(NHALF):
-            if sg == step_of_cda(h) + 1:
+            if sg == step_of_cda(h) + CDB_LAG:
                 add(("cdb", h))
                 add(("xs", h))
                 if h % 2 == 1:
@@ -54,7 +56,7 @@ def schedule():
                 add(("tm", b, 1))
                 add(("qt", b))
         for tau in range(NTILE):
-            if max(tau - SC_AHEAD, step_of_cda(tau // 4) + 1) == sg:
+            if max(tau - SC_AHEAD, step_of_cda(tau // 4) + CDB_LAG) == sg:
                 add(("sc", tau))
         if sg % 4 == 0 and 4 <= sg < NTILE:
             add(("q2", sg // 4 - 1, -1))
@@ -79,7 +81,6 @@ def schedule():
             add(("dmm", t1_tile - 1))
         for h in range(NHALF):
             if sg == step_of_cda(h):
-                add(("cda", h))
                 add(("cds", h))
         for b in range(B):
             if m1s[b] <= sg < m1s[b] + 4:
@@ -114,15 +115,19 @@ def tile_hgcn_t_kernel(tc, node_features, hyper_graph, W_line, out):
 
         ident = const.tile([P, P], BF16)
         make_identity(nc, ident[:])
-        wzb = const.tile([P, 2048], BF16, align_bytes=64)
-        nc.vector.memset(wzb[:], 0.0)
-        wz = const.tile([P, 512], U32, align_bytes=64)
-        wzs = const.tile([P, 512], U8, align_bytes=64)
-        nc.vector.quantize_mx(out=wz[:].bitcast(FP8X4), scales=wzs[:], in_=wzb[:])
-        ones = const.tile([P, ND], BF16)
-        nc.vector.memset(ones[:], 1.0)
         wrows = const.tile([P, P], BF16)
         nc.vector.memset(wrows[:], 0.0)
+        wzb = const.tile([P, 512], BF16, align_bytes=64)
+        nc.vector.memset(wzb[:], 0.0)
+        wz = const.tile([P, P], U32, align_bytes=64)
+        wzs = const.tile([P, P], U8, align_bytes=64)
+        nc.vector.quantize_mx(out=wz[:].bitcast(FP8X4), scales=wzs[:], in_=wzb[:])
+        tiny = const.tile([P, 1], F32)
+        nc.vector.memset(tiny[:], TINY)
+        ones = const.tile([P, ND], BF16)
+        nc.vector.memset(ones[:], 1.0)
+        tiny_sq = const.tile([P, 1], F32)
+        nc.scalar.activation(out=tiny_sq[:], in_=tiny[:], func=ACT.Sqrt, bias=tiny[:], scale=1.0)
         nc.sync.dma_start(out=wrows[0:NT, :], in_=W_line.rearrange("(s m) -> s m", m=P))
 
         raw = {}
@@ -142,12 +147,12 @@ def tile_hgcn_t_kernel(tc, node_features, hyper_graph, W_line, out):
                     out=xraw[b][:], in_=node_features[b].rearrange("(c p j) f -> p c j f", c=2, j=PACK)
                 )
 
-        warm_ps = psum.tile([P, 512], F32, tag="mm", bufs=2, name="warm_ps")
+        warm_ps = psum.tile([P, P], F32, tag="mm", bufs=2, name="warm_ps")
         for i in range(NWARM):
             nc.tensor.matmul_mx(
                 out=warm_ps[:],
-                lhsT=wz[:, 0:P].bitcast(FP8X4),
-                lhsT_scale=wzs[:, 0:P],
+                lhsT=wz[:].bitcast(FP8X4),
+                lhsT_scale=wzs[:],
                 rhs=wz[:].bitcast(FP8X4),
                 rhs_scale=wzs[:],
                 start=True,
@@ -209,17 +214,12 @@ def tile_hgcn_t_kernel(tc, node_features, hyper_graph, W_line, out):
                     nc.tensor.matmul(
                         deg[:, j, :], lhsT=ht[:, j, s, :], rhs=wrep[:, s, :], start=(s == 0), stop=(s == NT - 1)
                     )
-            elif k == "cda":
-                h = o[1]
-                nz = small.tile([P, PACK], F32, name="d_nz")
-                nc.vector.tensor_scalar(
-                    out=nz[:], in0=st[("deg", h)][:, 0:PACK, 0], scalar1=TINY, scalar2=None, op0=ALU.max
-                )
-                st[("nz", h)] = nz
             elif k == "cds":
                 h = o[1]
                 sq = small.tile([P, PACK], F32, name="d_sq")
-                nc.scalar.sqrt(out=sq[:], in_=st[("nz", h)][:])
+                nc.scalar.activation(
+                    out=sq[:], in_=st[("deg", h)][:, 0:PACK, 0], func=ACT.Sqrt, bias=tiny[:], scale=1.0
+                )
                 st[("sq", h)] = sq
                 bsb = small.tile([P, NT], F32, name="b_part")
                 nc.scalar.copy(out=bsb[:], in_=st[("deg", h)][:, PACK : PACK + NT, 0])

@@ -100,7 +100,6 @@ def schedule():
 def tile_hgcn_t_kernel(tc, node_features, hyper_graph, W_line, out):
     nc = tc.nc
     with ExitStack() as ctx:
-        ctx.enter_context(tc.manual_schedule())
         const = ctx.enter_context(tc.tile_pool(name="const", bufs=1))
         rawp = ctx.enter_context(tc.tile_pool(name="rawp", bufs=1))
         htp = ctx.enter_context(tc.tile_pool(name="htp", bufs=2))

@@ -22,7 +22,6 @@ LEAD = 8
 SC_AHEAD = 2
 M1_LAG = 3
 CDB_LAG = 2
-NWARM = 12
 TINY = 2.0 ** -100
 
 FLOPS = 2 * 2 * B * N * E * F
@@ -116,11 +115,6 @@ def tile_hgcn_t_kernel(tc, node_features, hyper_graph, W_line, out):
         make_identity(nc, ident[:])
         wrows = const.tile([P, P], BF16)
         nc.vector.memset(wrows[:], 0.0)
-        wzb = const.tile([P, 512], BF16, align_bytes=64)
-        nc.vector.memset(wzb[:], 0.0)
-        wz = const.tile([P, P], U32, align_bytes=64)
-        wzs = const.tile([P, P], U8, align_bytes=64)
-        nc.vector.quantize_mx(out=wz[:].bitcast(FP8X4), scales=wzs[:], in_=wzb[:])
         tiny = const.tile([P, 1], F32)
         nc.vector.memset(tiny[:], TINY)
         ones = const.tile([P, ND], BF16)
@@ -145,18 +139,6 @@ def tile_hgcn_t_kernel(tc, node_features, hyper_graph, W_line, out):
                 nc.sync.dma_start(
                     out=xraw[b][:], in_=node_features[b].rearrange("(c p j) f -> p c j f", c=2, j=PACK)
                 )
-
-        warm_ps = psum.tile([P, P], F32, tag="mm", bufs=2, name="warm_ps")
-        for i in range(NWARM):
-            nc.tensor.matmul_mx(
-                out=warm_ps[:],
-                lhsT=wz[:].bitcast(FP8X4),
-                lhsT_scale=wzs[:],
-                rhs=wz[:].bitcast(FP8X4),
-                rhs_scale=wzs[:],
-                start=True,
-                stop=True,
-            )
 
         wt_ps = psum.tile([P, PACK, P], BF16, tag="tp", bufs=4, name="wt_ps")
         nc.tensor.transpose(wt_ps[:, 0, :], wrows[:], ident[:])

from contextlib import ExitStack

import concourse.mybir as mybir
from concourse.masks import make_identity

FP8X4 = mybir.dt.float8_e4m3fn_x4
BF16 = mybir.dt.bfloat16
F32 = mybir.dt.float32
U32 = mybir.dt.uint32
U8 = mybir.dt.uint8
ALU = mybir.AluOpType
ACT = mybir.ActivationFunctionType

B, N, E, F = 4, 1024, 1024, 128
P = 128
PACK = 4
NT = 8
NHALF = 8
NTILE = 32
ND = 12
LEAD = 8
SC_AHEAD = 2
M1_LAG = 3
CDB_LAG = 2
TINY = 2.0 ** -100

FLOPS = 2 * 2 * B * N * E * F


def schedule():
    ops = []
    add = ops.append

    def step_of_cda(h):
        return 4 * h + 4 - LEAD

    m1s = [max(step_of_cda(2 * b + 1) + M1_LAG, 0) for b in range(B)]
    m2s = {}
    for b in range(B):
        m2s[2 * b] = max(m1s[b] + 5, 8 * b + 5)
        m2s[2 * b + 1] = max(m2s[2 * b] + 2, 8 * b + 9)
    last = max(m2s.values()) + 3
    for sg in range(-LEAD, last):
        t1_tile = sg + LEAD
        for h in range(NHALF):
            if sg == step_of_cda(h) + CDB_LAG:
                add(("cdb", h))
                add(("xs", h))
                if h % 2 == 1:
                    add(("qx", h // 2))
        for b in range(B):
            if sg == m1s[b] + 2:
                add(("tm", b, 0))
            if sg == m1s[b] + 4:
                add(("tm", b, 1))
                add(("qt", b))
        for tau in range(NTILE):
            if max(tau - SC_AHEAD, step_of_cda(tau // 4) + CDB_LAG) == sg:
                add(("sc", tau))
        if sg % 4 == 0 and 4 <= sg < NTILE:
            add(("q2", sg // 4 - 1, -1))
        h, r = t1_tile // 4, t1_tile % 4
        if 0 <= h < NHALF:
            if r == 1:
                add(("r1", h, 0))
            elif r == 2:
                add(("r1", h, 1))
            elif r == 3:
                add(("q1", h))
        for b in range(B):
            if sg == m1s[b]:
                add(("cb", b))
        if 0 <= sg < NTILE:
            add(("t2", sg))
            if sg >= NTILE - 4:
                add(("q2", NHALF - 1, sg % 4))
        if 0 <= t1_tile < NTILE:
            add(("t1", t1_tile))
        if 0 <= t1_tile - 1 < NTILE:
            add(("dmm", t1_tile - 1))
        for h in range(NHALF):
            if sg == step_of_cda(h):
                add(("cds", h))
        for b in range(B):
            if m1s[b] <= sg < m1s[b] + 4:
                add(("m1", b, 2 * (sg - m1s[b])))
                add(("m1", b, 2 * (sg - m1s[b]) + 1))
        for h in range(NHALF):
            if m2s[h] <= sg < m2s[h] + 2:
                add(("m2", 4 * h + 2 * (sg - m2s[h])))
                add(("m2", 4 * h + 2 * (sg - m2s[h]) + 1))
            if sg == m2s[h] + 1:
                add(("eo", h))
        if 0 <= t1_tile < NTILE:
            add(("bmm", t1_tile // 4, t1_tile % 4))
    return ops


def tile_hgcn_t_kernel(tc, node_features, hyper_graph, W_line, out):
    nc = tc.nc
    with ExitStack() as ctx:
        const = ctx.enter_context(tc.tile_pool(name="const", bufs=1))
        rawp = ctx.enter_context(tc.tile_pool(name="rawp", bufs=1))
        htp = ctx.enter_context(tc.tile_pool(name="htp", bufs=2))
        hsp = ctx.enter_context(tc.tile_pool(name="hsp", bufs=2))
        g1p = ctx.enter_context(tc.tile_pool(name="g1p", bufs=2))
        g2p = ctx.enter_context(tc.tile_pool(name="g2p", bufs=2))
        qp = ctx.enter_context(tc.tile_pool(name="qp", bufs=2))
        small = ctx.enter_context(tc.tile_pool(name="small", bufs=4))
        xp = ctx.enter_context(tc.tile_pool(name="xp", bufs=2))
        op = ctx.enter_context(tc.tile_pool(name="op", bufs=3))
        psum = ctx.enter_context(tc.psum_pool(name="psum", bufs=1))

        ident = const.tile([P, P], BF16)
        make_identity(nc, ident[:])
        wrows = const.tile([P, P], BF16)
        nc.vector.memset(wrows[:], 0.0)
        tiny = const.tile([P, 1], F32)
        nc.vector.memset(tiny[:], TINY)
        ones = const.tile([P, ND], BF16)
        nc.vector.memset(ones[:], 1.0)
        tiny_sq = const.tile([P, 1], F32)
        nc.scalar.activation(out=tiny_sq[:], in_=tiny[:], func=ACT.Sqrt, bias=tiny[:], scale=1.0)
        nc.sync.dma_start(out=wrows[0:NT, :], in_=W_line.rearrange("(s m) -> s m", m=P))

        raw = {}
        xraw = {}
        for h in range(NHALF):
            b, c = h // 2, h % 2
            raw[h] = rawp.tile([P, PACK, E], BF16, name="raw%d" % h)
            src = hyper_graph[b, c * 512 : (c + 1) * 512, :].rearrange("(p j) e -> p j e", j=PACK)
            if h == 0:
                for j in range(PACK):
                    nc.sync.dma_start(out=raw[h][:, j, :], in_=src[:, j, :])
            else:
                nc.sync.dma_start(out=raw[h][:], in_=src)
            if c == 1:
                xraw[b] = rawp.tile([P, 2, PACK, F], BF16, name="xraw%d" % b)
                nc.sync.dma_start(
                    out=xraw[b][:], in_=node_features[b].rearrange("(c p j) f -> p c j f", c=2, j=PACK)
                )

        wt_ps = psum.tile([P, PACK, P], BF16, tag="tp", bufs=4, name="wt_ps")
        nc.tensor.transpose(wt_ps[:, 0, :], wrows[:], ident[:])
        wsb = const.tile([P, NT], F32)
        nc.vector.tensor_copy(out=wsb[:], in_=wt_ps[:, 0, 0:NT])
        wabs_f = const.tile([P, NT], F32)
        nc.vector.scalar_tensor_tensor(
            out=wabs_f[:], in0=wsb[:], scalar=-1.0, in1=wsb[:], op0=ALU.mult, op1=ALU.max
        )
        wrep = const.tile([P, NT, ND], BF16)
        nc.vector.tensor_copy(out=wrep[:], in_=wabs_f[:].unsqueeze(2).to_broadcast([P, NT, ND]))

        st = {}

        def transposes(src_tile, j, g, nm):
            tp = psum.tile([P, PACK, P], BF16, tag="tp", bufs=4, name=nm)
            for t in range(PACK):
                s = g * PACK + t
                nc.tensor.transpose(tp[:, t, :], src_tile[:, j, s * P : (s + 1) * P], ident[:])
            return tp

        for o in schedule():
            k = o[0]
            if k == "t1":
                h, j = o[1] // 4, o[1] % 4
                if j == 0:
                    st[("ht", h)] = htp.tile([P, PACK, NT, P], BF16, name="ht")
                ht = st[("ht", h)]
                for g in range(2):
                    tp = transposes(raw[h], j, g, "tp1")
                    nc.scalar.copy(
                        out=ht[:, j, g * PACK : (g + 1) * PACK, :].rearrange("m s p -> m (s p)").bitcast(F32),
                        in_=tp[:].rearrange("m s p -> m (s p)").bitcast(F32),
                    )
            elif k == "bmm":
                h, r = o[1], o[2]
                if r == 0:
                    st[("deg", h)] = psum.tile([P, PACK + NT, ND], F32, tag="deg", bufs=2, name="deg")
                deg = st[("deg", h)]
                for s in (2 * r, 2 * r + 1):
                    for j in range(PACK):
                        nc.tensor.matmul(
                            deg[:, PACK + s, :],
                            lhsT=raw[h][:, j, s * P : (s + 1) * P],
                            rhs=ones[:],
                            start=(j == 0),
                            stop=(j == PACK - 1),
                        )
            elif k == "dmm":
                h, j = o[1] // 4, o[1] % 4
                deg = st[("deg", h)]
                ht = st[("ht", h)]
                for s in range(NT):
                    nc.tensor.matmul(
                        deg[:, j, :], lhsT=ht[:, j, s, :], rhs=wrep[:, s, :], start=(s == 0), stop=(s == NT - 1)
                    )
            elif k == "cds":
                h = o[1]
                sq = small.tile([P, PACK], F32, name="d_sq")
                nc.scalar.activation(
                    out=sq[:], in_=st[("deg", h)][:, 0:PACK, 0], func=ACT.Sqrt, bias=tiny[:], scale=1.0
                )
                st[("sq", h)] = sq
                bsb = small.tile([P, NT], F32, name="b_part")
                nc.scalar.copy(out=bsb[:], in_=st[("deg", h)][:, PACK : PACK + NT, 0])
                st[("bsb", h)] = bsb
            elif k == "cdb":
                h = o[1]
                rc = small.tile([P, PACK], F32, name="d_rc")
                nc.vector.reciprocal(out=rc[:], in_=st[("sq", h)][:])
                dinv = small.tile([P, PACK], F32, name="d_inv")
                nc.vector.scalar_tensor_tensor(
                    out=dinv[:], in0=st[("deg", h)][:, 0:PACK, 0], scalar=0.0, in1=rc[:], op0=ALU.is_gt, op1=ALU.mult
                )
                st[("dinv", h)] = dinv
            elif k == "cb":
                b = o[1]
                bs = small.tile([P, NT], F32, name="b_sum")
                nc.vector.tensor_tensor(
                    out=bs[:], in0=st[("bsb", 2 * b)][:], in1=st[("bsb", 2 * b + 1)][:], op=ALU.add
                )
                bnz = small.tile([P, NT], F32, name="b_nz")
                nc.vector.scalar_tensor_tensor(
                    out=bnz[:], in0=bs[:], scalar=0.0, in1=bs[:], op0=ALU.is_equal, op1=ALU.add
                )
                brc = small.tile([P, NT], F32, name="b_rc")
                nc.vector.reciprocal(out=brc[:], in_=bnz[:])
                binv = small.tile([P, NT], F32, name="b_inv")
                nc.vector.scalar_tensor_tensor(
                    out=binv[:], in0=bs[:], scalar=0.0, in1=brc[:], op0=ALU.not_equal, op1=ALU.mult
                )
                wb = small.tile([P, NT], F32, name="wb")
                nc.vector.tensor_tensor(out=wb[:], in0=binv[:], in1=wabs_f[:], op=ALU.mult)
                st[("wb", b)] = wb
            elif k == "xs":
                h = o[1]
                b, c = h // 2, h % 2
                if c == 0:
                    st[("xg", b)] = xp.tile([P, 2, F, PACK], BF16, name="xg", align_bytes=64)
                nc.vector.tensor_tensor(
                    out=st[("xg", b)][:, c, :, :],
                    in0=xraw[b][:, c, :, :].rearrange("p j f -> p f j"),
                    in1=st[("dinv", h)][:].unsqueeze(1).to_broadcast([P, F, PACK]),
                    op=ALU.mult,
                )
            elif k == "qx":
                b = o[1]
                xq = xp.tile([P, 2 * F], U32, name="xq", align_bytes=64)
                xs = xp.tile([P, 2 * F], U8, name="xs", align_bytes=64)
                nc.vector.quantize_mx(
                    out=xq[:].bitcast(FP8X4), scales=xs[:], in_=st[("xg", b)][:].rearrange("p c f j -> p (c f j)")
                )
                st[("xq", b)] = (xq, xs)
            elif k == "sc":
                h, j = o[1] // 4, o[1] % 4
                if j == 0:
                    st[("hs", h)] = hsp.tile([P, PACK, E], BF16, name="hs")
                nc.vector.tensor_scalar(
                    out=st[("hs", h)][:, j, :],
                    in0=raw[h][:, j, :],
                    scalar1=st[("dinv", h)][:, j : j + 1],
                    scalar2=None,
                    op0=ALU.mult,
                )
            elif k == "t2":
                h, j = o[1] // 4, o[1] % 4
                if j == 0:
                    st[("g2", h)] = g2p.tile([P, PACK, 2, P, PACK], BF16, name="g2", align_bytes=64)
                for g in range(2):
                    tp = transposes(st[("hs", h)], j, g, "tp2")
                    nc.scalar.copy(out=st[("g2", h)][:, j, g, :, :], in_=tp[:].rearrange("m t p -> m p t"))
            elif k == "q2":
                h, j = o[1], o[2]
                if j <= 0:
                    codes2 = qp.tile([P, PACK * 2 * P], U32, name="codes2", align_bytes=64)
                    scales2 = qp.tile([P, PACK * 2 * P], U8, name="scales2", align_bytes=64)
                    st[("q2", h)] = (codes2, scales2)
                codes2, scales2 = st[("q2", h)]
                if j < 0:
                    nc.vector.quantize_mx(
                        out=codes2[:].bitcast(FP8X4),
                        scales=scales2[:],
                        in_=st[("g2", h)][:].rearrange("m j g p t -> m (j g p t)"),
                    )
                else:
                    w = 2 * P
                    nc.vector.quantize_mx(
                        out=codes2[:, j * w : (j + 1) * w].bitcast(FP8X4),
                        scales=scales2[:, j * w : (j + 1) * w],
                        in_=st[("g2", h)][:, j, :, :, :].rearrange("m g p t -> m (g p t)"),
                    )
            elif k == "r1":
                h, x = o[1], o[2]
                if x == 0:
                    st[("g1", h)] = g1p.tile([P, E, PACK], BF16, name="g1", align_bytes=64)
                e0, e1 = x * 512, (x + 1) * 512
                nc.vector.tensor_copy(
                    out=st[("g1", h)][:, e0:e1, :].rearrange("p (c i) t -> p c t i", i=4),
                    in_=raw[h][:, :, e0:e1].rearrange("p t (c i) -> p c t i", i=4),
                )
            elif k == "q1":
                h = o[1]
                b, c = h // 2, h % 2
                if c == 0:
                    codes1 = qp.tile([P, 2, E], U32, name="codes1", align_bytes=64)
                    scales1 = qp.tile([P, 2, E], U8, name="scales1", align_bytes=64)
                    st[("q1", b)] = (codes1, scales1)
                codes1, scales1 = st[("q1", b)]
                nc.vector.quantize_mx(
                    out=codes1[:, c, :].bitcast(FP8X4),
                    scales=scales1[:, c, :],
                    in_=st[("g1", h)][:].rearrange("p e j -> p (e j)"),
                )
            elif k == "m1":
                b, s = o[1], o[2]
                g, t = s // PACK, s % PACK
                if t == 0:
                    st[("tmp", b, g)] = psum.tile([P, PACK, F], F32, tag="mm", bufs=2, name="tmp_ps")
                codes1, scales1 = st[("q1", b)]
                xq, xs = st[("xq", b)]
                for c in range(2):
                    nc.tensor.matmul_mx(
                        out=st[("tmp", b, g)][:, t, :],
                        lhsT=codes1[:, c, s * P : (s + 1) * P].bitcast(FP8X4),
                        lhsT_scale=scales1[:, c, s * P : (s + 1) * P],
                        rhs=xq[:, c * F : (c + 1) * F].bitcast(FP8X4),
                        rhs_scale=xs[:, c * F : (c + 1) * F],
                        start=(c == 0),
                        stop=(c == 1),
                    )
            elif k == "tm":
                b, g = o[1], o[2]
                if g == 0:
                    st[("t2g", b)] = xp.tile([P, 2, F, PACK], BF16, name="t2g", align_bytes=64)
                nc.vector.tensor_tensor(
                    out=st[("t2g", b)][:, g, :, :],
                    in0=st[("tmp", b, g)][:].rearrange("m t f -> m f t"),
                    in1=st[("wb", b)][:, g * PACK : (g + 1) * PACK].unsqueeze(1).to_broadcast([P, F, PACK]),
                    op=ALU.mult,
                )
            elif k == "qt":
                b = o[1]
                t2q = xp.tile([P, 2 * F], U32, name="t2q", align_bytes=64)
                t2s = xp.tile([P, 2 * F], U8, name="t2s", align_bytes=64)
                nc.vector.quantize_mx(
                    out=t2q[:].bitcast(FP8X4), scales=t2s[:], in_=st[("t2g", b)][:].rearrange("p g f t -> p (g f t)")
                )
                st[("t2q", b)] = (t2q, t2s)
            elif k == "m2":
                h, j = o[1] // 4, o[1] % 4
                if j == 0:
                    st[("o", h)] = psum.tile([P, PACK, F], F32, tag="mm", bufs=2, name="o_ps")
                codes2, scales2 = st[("q2", h)]
                t2q, t2s = st[("t2q", h // 2)]
                for g in range(2):
                    q = (j * 2 + g) * P
                    nc.tensor.matmul_mx(
                        out=st[("o", h)][:, j, :],
                        lhsT=codes2[:, q : q + P].bitcast(FP8X4),
                        lhsT_scale=scales2[:, q : q + P],
                        rhs=t2q[:, g * F : (g + 1) * F].bitcast(FP8X4),
                        rhs_scale=t2s[:, g * F : (g + 1) * F],
                        start=(g == 0),
                        stop=(g == 1),
                    )
            elif k == "eo":
                h = o[1]
                b, c = h // 2, h % 2
                osb = op.tile([P, PACK, F], F32, name="osb")
                nc.scalar.copy(out=osb[:], in_=st[("o", h)][:])
                nc.sync.dma_start(
                    out=out[b, c * 512 : (c + 1) * 512, :].rearrange("(p j) f -> p j f", j=PACK), in_=osb[:]
                )
